import numpy as np
import ml_dtypes


def mxq(x, axis, fmt="e4m3"):
    dtype, down = {"e4m3": (ml_dtypes.float8_e4m3fn, 7), "e5m2": (ml_dtypes.float8_e5m2, 14)}[fmt]
    v = np.moveaxis(np.asarray(x, np.float32).astype(ml_dtypes.bfloat16).astype(np.float64), axis, -1)
    blocks = v.reshape(v.shape[:-1] + (-1, 32))
    amax = np.abs(blocks).max(-1, keepdims=True)
    byte = np.maximum(np.where(amax > 0, np.frexp(amax)[1] - 1 + 127, 0) - down, 1)
    scale = np.exp2(byte - 127.0)
    codes = (blocks / scale).astype(np.float32).astype(dtype).astype(np.float64)
    return np.moveaxis((codes * scale).reshape(v.shape), -1, axis)


WIDE = False


def mx_kscale(k):
    if not WIDE:
        return np.ones(k)
    levels = np.array([10, -10, 5, -5, 0])
    if k % 512:
        return np.exp2(np.random.permutation(np.resize(levels, k // 32))).repeat(32)
    a = np.empty((k // 512, 16))
    for p in range(k // 512):
        a[p, :8] = np.random.permutation(np.resize(levels, 8))
        for g in range(8):
            far = levels[np.abs(levels - a[p, g]) >= 10]
            a[p, g + 8] = far[np.random.randint(len(far))]
    return np.exp2(a.ravel()).repeat(32)


BF16 = ml_dtypes.bfloat16


def bf(x):
    return np.asarray(x, np.float32).astype(BF16)


def f64(x):
    return np.asarray(x).astype(np.float64)


B, H, HKV, S, D = 8, 4, 2, 512, 256
G = H // HKV
NEG = -1e9


def setup_inputs():
    s = mx_kscale(S)
    keep = np.random.random((B, 1, S, S)) < 0.75
    return {"query": bf(np.random.standard_normal((B, H, S, D))),
            "key": bf(np.random.standard_normal((B, HKV, S, D))),
            "value": bf(np.random.standard_normal((B, HKV, S, D)) * 0.25 * np.sqrt(S) * s.max() / s[:, None]),
            "attention_mask": bf(np.where(keep, 0.5 * np.random.standard_normal((B, 1, S, S)) + np.log(s), NEG)),
            "sinks": bf(np.log(S * s.max()) - 3.5 + np.random.standard_normal(H))}


def reference(query, key, value, attention_mask, sinks):
    scaling = 1.0 / np.sqrt(D)
    k = np.repeat(f64(key), G, axis=1)
    attn = (f64(query) @ k.transpose(0, 1, 3, 2)) * scaling
    attn = attn + f64(attention_mask)[:, :, :, :attn.shape[-1]]
    sink_col = np.broadcast_to(f64(sinks).reshape(1, H, 1, 1), (B, H, S, 1))
    combined = np.concatenate([attn, sink_col], axis=-1)
    combined = combined - combined.max(-1, keepdims=True)
    e = np.exp(combined[..., :-1])
    den = e.sum(-1, keepdims=True) + np.exp(combined[..., -1:])
    eg = e.reshape(B, HKV, G * S, S)
    pv = mxq(eg, 3, "e4m3") @ mxq(f64(value), 2, "e4m3")
    out = pv.reshape(B, H, S, D) / den
    return out.transpose(0, 2, 1, 3)

@@ -1,0 +1,449 @@
+from contextlib import ExitStack
+
+import concourse.mybir as mybir
+from concourse.masks import make_identity
+
+F32 = mybir.dt.float32
+BF16 = mybir.dt.bfloat16
+U32 = mybir.dt.uint32
+U8 = mybir.dt.uint8
+FP8X4 = mybir.dt.float8_e4m3fn_x4
+ALU = mybir.AluOpType
+ACT = mybir.ActivationFunctionType
+AX = mybir.AxisListType
+
+B, H, HKV, S, D = 8, 4, 2, 512, 256
+G = H // HKV
+P = 128
+NT = S // P
+W = D // 2
+SCALE = 1.0 / 16.0
+ROW = 520
+UNITS_PER_BATCH = H * NT // 2
+N_UNITS = B * UNITS_PER_BATCH
+TILE_E = P * NT
+DEN_STEP = 8
+N_DIRECT = 2
+WORD_GROUPS = (("k", 0), ("q", 0), ("q", 1), ("k", 1), ("q", 2), ("q", 3))
+FIRST_NEED = {0: (0, 1), 1: (2,), 2: (3, 4), 3: (5,)}
+FIRST_GROUP_ROUND = 2
+FLOPS = 2 * 2 * B * H * S * S * D
+
+
+def tile_deepseekv4attention_t_kernel(tc, query, key, value, attention_mask, sinks, out):
+    nc = tc.nc
+    with ExitStack() as ctx:
+        const = ctx.enter_context(tc.tile_pool(name="const", bufs=1))
+        ld = ctx.enter_context(tc.tile_pool(name="ld", bufs=3))
+        prep = ctx.enter_context(tc.tile_pool(name="prep", bufs=2))
+        prep3 = ctx.enter_context(tc.tile_pool(name="prep3", bufs=3))
+        work = ctx.enter_context(tc.tile_pool(name="work", bufs=3))
+        work4 = ctx.enter_context(tc.tile_pool(name="work4", bufs=4))
+        one = ctx.enter_context(tc.tile_pool(name="one", bufs=1))
+        stat = ctx.enter_context(tc.tile_pool(name="stat", bufs=6))
+        outp = ctx.enter_context(tc.tile_pool(name="outp", bufs=3))
+        ps_sc = ctx.enter_context(tc.psum_pool(name="ps_sc", bufs=4))
+        ps_et = ctx.enter_context(tc.psum_pool(name="ps_et", bufs=2))
+        ps_o = ctx.enter_context(tc.psum_pool(name="ps_o", bufs=1))
+        ps_tq = ctx.enter_context(tc.psum_pool(name="ps_tq", bufs=1))
+        ctx.enter_context(tc.manual_schedule())
+
+        loaded = {}
+        ready = {}
+        st = {}
+
+        def valid(n):
+            return 0 <= n < N_UNITS
+
+        def where(n):
+            b, j = divmod(n, UNITS_PER_BATCH)
+            tp, h = divmod(j, H)
+            return b, tp, h
+
+        def mask_on_pe(n):
+            b, j = divmod(n, UNITS_PER_BATCH)
+            return j == UNITS_PER_BATCH - 1 or (j == 3 and b % 2 == 0)
+
+        def mask_tile(b, t):
+            return loaded[b]["m"][:, t * S : (t + 1) * S].rearrange("p (w t) -> p t w", t=NT)
+
+        def direct(n):
+            return n >= N_UNITS - N_DIRECT
+
+
+        def load(b, fine):
+            k_sb = ld.tile([P, HKV * NT * D], BF16, tag="k_sb")
+            q_sb = ld.tile([P, H * NT * D], BF16, tag="q_sb")
+            m_sb = ld.tile([P, NT * S], BF16, tag="m_sb")
+            v_sb = ld.tile([P, HKV * NT * D], BF16, tag="v_sb")
+            loaded[b] = {"q": q_sb, "k": k_sb, "v": v_sb, "m": m_sb}
+            blk = NT * D
+
+            def load_k(g0, g1):
+                nc.sync.dma_start(
+                    out=k_sb[:, g0 * blk : g1 * blk].rearrange("p (g x) -> p g x", x=blk),
+                    in_=key[b, g0:g1].rearrange("g (p t) d -> p g (t d)", t=NT),
+                )
+
+            def load_q(h0, h1):
+                nc.sync.dma_start(
+                    out=q_sb[:, h0 * blk : h1 * blk].rearrange("p (h x) -> p h x", x=blk),
+                    in_=query[b, h0:h1].rearrange("h (p t) d -> p h (t d)", t=NT),
+                )
+
+            def load_m(t0, t1):
+                nc.sync.dma_start(
+                    out=m_sb[:, t0 * S : t1 * S],
+                    in_=attention_mask[b, 0].rearrange("(p t) k -> p t k", t=NT)[:, t0:t1, :].rearrange("p t k -> p (t k)"),
+                )
+
+            if fine:
+                load_k(0, 1)
+                load_q(0, 1)
+                load_m(0, 2)
+                load_q(1, 2)
+                load_k(1, 2)
+                load_q(2, 3)
+                load_q(3, 4)
+                load_m(2, NT)
+            else:
+                load_k(0, HKV)
+                load_q(0, H)
+                load_m(0, NT)
+            nc.sync.dma_start(
+                out=v_sb[:].rearrange("p (g x) -> p g x", x=blk),
+                in_=value[b].rearrange("g (p t) d -> p g (t d)", t=NT),
+            )
+
+
+        def prep_alloc(b):
+            qT = prep.tile([P, H * NT * P], F32, tag="qT")
+            kT = prep.tile([P, HKV * NT * P], F32, tag="kT")
+            vg = prep.tile([P, HKV * D * NT], BF16, tag="vg", align_bytes=64)
+            vc = prep3.tile([P, HKV * D], U32, tag="vc", align_bytes=64)
+            vs = prep3.tile([P, HKV * D], U8, tag="vs", align_bytes=64)
+            ready[b] = {"q": qT, "k": kT, "vg": vg, "vc": vc, "vs": vs}
+
+        def words_transpose(b, c):
+            if b >= B or not 0 <= c < len(WORD_GROUPS):
+                return
+            which, blk = WORD_GROUPS[c]
+            src = loaded[b][which]
+            tq = ps_tq.tile([P, NT, P], F32, tag="tq")
+            for t in range(NT):
+                c0 = (blk * NT + t) * W
+                nc.tensor.transpose(tq[:, t, :], src[:].bitcast(F32)[:, c0 : c0 + W], ident_f[:])
+            st[(b, "tq", c)] = tq
+
+        def words_copy(b, c, on_vector):
+            if b >= B or not 0 <= c < len(WORD_GROUPS):
+                return
+            which, blk = WORD_GROUPS[c]
+            dst_cols = ready[b][which][:, blk * NT * P : (blk + 1) * NT * P]
+            tq = st[(b, "tq", c)]
+            if on_vector:
+                nc.vector.tensor_copy(out=dst_cols, in_=tq[:].rearrange("p t q -> p (t q)"))
+            else:
+                nc.scalar.copy(out=dst_cols, in_=tq[:].rearrange("p t q -> p (t q)"))
+
+        def value_group(b, g):
+            if b >= B:
+                return
+            cols = slice(g * D * NT, (g + 1) * D * NT)
+            nc.vector.tensor_copy(
+                out=ready[b]["vg"][:, cols].rearrange("p (c i t) -> p c t i", i=4, t=NT),
+                in_=loaded[b]["v"][:, cols].rearrange("p (t c i) -> p c t i", i=4, t=NT),
+            )
+
+        def value_quant(b):
+            if b >= B:
+                return
+            r = ready[b]
+            nc.vector.quantize_mx(out=r["vc"][:].bitcast(FP8X4), scales=r["vs"][:], in_=r["vg"][:])
+
+
+        def qk(n, i):
+            if not valid(n):
+                return
+            b, tp, h = where(n)
+            g = h // G
+            t = 2 * tp + i
+            qTb = ready[b]["q"][:].bitcast(BF16).rearrange("p (c e) -> p c e", e=2)
+            kTb = ready[b]["k"][:].bitcast(BF16).rearrange("p (c e) -> p c e", e=2)
+            sc = ps_sc.tile([P, S], F32, tag="sc")
+            c0 = (h * NT + t) * P
+            on_pe = mask_on_pe(n)
+            if on_pe:
+                nc.tensor.matmul(
+                    sc[:].rearrange("p (t w) -> p t w", t=NT), lhsT=ident16[:], rhs=mask_tile(b, t), start=True, stop=False
+                )
+            for e in range(2):
+                nc.tensor.matmul(
+                    sc[:],
+                    lhsT=qTb[:, c0 : c0 + P, e],
+                    rhs=kTb[:, g * S : (g + 1) * S, e],
+                    start=(e == 0 and not on_pe),
+                    stop=(e == 1),
+                )
+            st[(n, "sc", i)] = sc
+
+        def add_mask(n, i):
+            if not valid(n):
+                return
+            b, tp, h = where(n)
+            t = 2 * tp + i
+            if mask_on_pe(n):
+                if i == 0:
+                    nm16 = stat.tile([P, 2], F32, tag="nm16")
+                    st[(n, "nm16")] = nm16
+                nc.vector.tensor_reduce(
+                    out=st[(n, "nm16")][:, i : i + 1], in_=st[(n, "sc", i)][:], axis=AX.X, op=ALU.max, negate=True
+                )
+                return
+            nc.vector.scalar_tensor_tensor(
+                out=s_bufs[h][:, i, 0:S].rearrange("p (t w) -> p t w", t=NT),
+                in0=st[(n, "sc", i)][:].rearrange("p (t w) -> p t w", t=NT),
+                scalar=SCALE,
+                in1=mask_tile(b, t),
+                op0=ALU.mult,
+                op1=ALU.add,
+            )
+
+        def row_max(n):
+            if not valid(n):
+                return
+            b, tp, h = where(n)
+            negm = stat.tile([P, 2], F32, tag="negm")
+            if mask_on_pe(n):
+                nc.vector.tensor_scalar(
+                    out=negm[:],
+                    in0=st[(n, "nm16")][:],
+                    scalar1=SCALE,
+                    scalar2=nsink[:, h : h + 1],
+                    op0=ALU.mult,
+                    op1=ALU.min,
+                )
+            else:
+                nc.vector.tensor_reduce(
+                    out=negm[:], in_=s_bufs[h][:, :, 0 : S + 1], axis=AX.X, op=ALU.max, negate=True
+                )
+            st[(n, "negm")] = negm
+
+        def exps(n):
+            if not valid(n):
+                return
+            b, tp, h = where(n)
+            negm = st[(n, "negm")]
+            e_sb = work.tile([P, 2, ROW], BF16, tag="e_sb")
+            if n % 2 == 0:
+                den_pair = stat.tile([P, 2 * DEN_STEP], F32, tag="den_pair")
+                st[(n // 2, "den_pair")] = den_pair
+            c_den = (n % 2) * DEN_STEP
+            if mask_on_pe(n):
+                den = stat.tile([P, 2], F32, tag="den")
+            else:
+                den = st[(n // 2, "den_pair")][:, c_den : c_den + 2]
+            for i in range(2):
+                if mask_on_pe(n):
+                    nc.scalar.activation(
+                        out=e_sb[:, i, 0:S],
+                        in_=st[(n, "sc", i)][:],
+                        func=ACT.Exp,
+                        bias=negm[:, i : i + 1],
+                        scale=SCALE,
+                        accum_out=den[:, i : i + 1],
+                    )
+                else:
+                    nc.scalar.activation(
+                        out=e_sb[:, i, 0 : S + 1],
+                        in_=s_bufs[h][:, i, 0 : S + 1],
+                        func=ACT.Exp,
+                        bias=negm[:, i : i + 1],
+                        scale=1.0,
+                        accum_out=den[:, i : i + 1],
+                    )
+            if mask_on_pe(n):
+                sterm = stat.tile([P, 2], F32, tag="sterm")
+                nc.scalar.activation(out=sterm[:], in_=negm[:], func=ACT.Exp, bias=sink_f[:, h : h + 1], scale=1.0)
+                st[(n, "sterm")] = sterm
+            st[(n, "e")] = e_sb
+            st[(n, "den")] = den
+
+        def recip(n):
+            if not valid(n):
+                return
+            den_pair = st[(n // 2, "den_pair")]
+            c_den = (n % 2) * DEN_STEP
+            if mask_on_pe(n):
+                nc.vector.tensor_tensor(
+                    out=den_pair[:, c_den : c_den + 2], in0=st[(n, "den")][:], in1=st[(n, "sterm")][:], op=ALU.add
+                )
+            if n % 2 == 1:
+                rden = stat.tile([P, 2, 2], F32, tag="rden")
+                nc.vector.reciprocal(out=rden[:], in_=den_pair[:].rearrange("p (a x) -> p a x", x=DEN_STEP)[:, :, 0:2])
+                st[(n // 2, "rden")] = rden
+
+        def e_transposes(n):
+            if not valid(n):
+                return
+            e_sb = st[(n, "e")]
+            et = ps_et.tile([P, 2, NT, P], BF16, tag="et")
+            for i in range(2):
+                for t in range(NT):
+                    nc.tensor.transpose(et[:, i, t, :], e_sb[:, i, t * P : (t + 1) * P], ident_b[:])
+            st[(n, "et")] = et
+
+        def e_out_of_psum(n):
+            if not valid(n):
+                return
+            et = st[(n, "et")]
+            if direct(n):
+                gr_v = work.tile([P, 2 * TILE_E], BF16, tag="gr_v", align_bytes=64)
+                nc.vector.tensor_copy(
+                    out=gr_v[:].rearrange("p (i q t) -> p i q t", i=2, t=NT), in_=et[:].rearrange("p i t q -> p i q t")
+                )
+                st[(n, "gr")] = gr_v[:]
+                return
+            etc = work4.tile([P, 2 * TILE_E], BF16, tag="etc")
+            nc.scalar.copy(out=etc[:], in_=et[:].rearrange("p i t q -> p (i t q)"))
+            st[(n, "etc")] = etc
+
+        def e_regroup(n):
+            if not valid(n) or direct(n):
+                return
+            if n % 2 == 0:
+                gr = one.tile([P, 4 * TILE_E], BF16, tag="gr", align_bytes=64)
+                st[(n // 2, "gr_pair")] = gr
+            half = st[(n // 2, "gr_pair")][:, (n % 2) * 2 * TILE_E : (n % 2 + 1) * 2 * TILE_E]
+            nc.gpsimd.tensor_scalar(
+                out=half.rearrange("p (i q t) -> p i q t", i=2, t=NT),
+                in0=st[(n, "etc")][:].rearrange("p (i t q) -> p i q t", i=2, t=NT),
+                scalar1=1.0,
+                scalar2=0.0,
+                op0=ALU.mult,
+                op1=ALU.add,
+            )
+
+        def e_quant(n):
+            if not valid(n):
+                return
+            if n % 2 == 0:
+                ec = work.tile([P, 4 * P], U32, tag="ec", align_bytes=64)
+                es = work.tile([P, 4 * P], U8, tag="es", align_bytes=64)
+                st[(n // 2, "ec")] = ec
+                st[(n // 2, "es")] = es
+            ec = st[(n // 2, "ec")]
+            es = st[(n // 2, "es")]
+            if direct(n):
+                cols = slice((n % 2) * 2 * P, (n % 2 + 1) * 2 * P)
+                nc.vector.quantize_mx(out=ec[:, cols].bitcast(FP8X4), scales=es[:, cols], in_=st[(n, "gr")])
+            elif n % 2 == 1:
+                nc.vector.quantize_mx(out=ec[:].bitcast(FP8X4), scales=es[:], in_=st[(n // 2, "gr_pair")][:])
+
+        def pv(n):
+            if not valid(n):
+                return
+            b, tp, h = where(n)
+            g = h // G
+            vc = ready[b]["vc"]
+            vs = ready[b]["vs"]
+            ec = st[(n // 2, "ec")]
+            es = st[(n // 2, "es")]
+            o_ps = ps_o.tile([P, 2, D], F32, tag="o_ps")
+            for i in range(2):
+                cols = slice(((n % 2) * 2 + i) * P, ((n % 2) * 2 + i + 1) * P)
+                nc.tensor.matmul_mx(
+                    out=o_ps[:, i, :],
+                    lhsT=ec[:, cols].bitcast(FP8X4),
+                    lhsT_scale=es[:, cols],
+                    rhs=vc[:, g * D : (g + 1) * D].bitcast(FP8X4),
+                    rhs_scale=vs[:, g * D : (g + 1) * D],
+                    start=True,
+                    stop=True,
+                )
+            st[(n, "o")] = o_ps
+
+        def finish(n):
+            if not valid(n):
+                return
+            b, tp, h = where(n)
+            o_ps = st[(n, "o")]
+            rden = st[(n // 2, "rden")][:, n % 2, :]
+            if h == 0:
+                o_new = outp.tile([P, 2, H, D], F32, tag="o_sb")
+                st[(b, tp, "o_sb")] = o_new
+            o_sb = st[(b, tp, "o_sb")]
+            for i in range(2):
+                nc.scalar.activation(out=o_sb[:, i, h, :], in_=o_ps[:, i, :], func=ACT.Copy, scale=rden[:, i : i + 1])
+            if b == B - 1 and tp == 1:
+                nc.sync.dma_start(
+                    out=out[b].rearrange("(p t) h d -> p t h d", t=NT)[:, 2 * tp : 2 * tp + 2, h, :],
+                    in_=o_sb[:, :, h, :],
+                )
+            elif h == H - 1:
+                nc.sync.dma_start(
+                    out=out[b].rearrange("(p t) h d -> p t (h d)", t=NT)[:, 2 * tp : 2 * tp + 2, :],
+                    in_=o_sb[:].rearrange("p i h d -> p i (h d)"),
+                )
+
+
+        sink_raw = const.tile([P, H], BF16)
+        nc.scalar.dma_start(out=sink_raw[:], in_=sinks.partition_broadcast(P))
+        load(0, True)
+        load(1, False)
+        ident_f = const.tile([P, P], F32)
+        make_identity(nc, ident_f[:])
+        ident_b = const.tile([P, P], BF16)
+        make_identity(nc, ident_b[:])
+        ident16 = const.tile([P, P], BF16)
+        nc.vector.tensor_scalar(out=ident16[:], in0=ident_b[:], scalar1=1.0 / SCALE, scalar2=None, op0=ALU.mult)
+        sink_f = const.tile([P, H], F32)
+        nc.vector.tensor_copy(out=sink_f[:], in_=sink_raw[:])
+        nsink = const.tile([P, H], F32)
+        nc.vector.tensor_scalar(out=nsink[:], in0=sink_raw[:], scalar1=-1.0, scalar2=None, op0=ALU.mult)
+        s_bufs = []
+        for h in range(H):
+            s_h = const.tile([P, 2, ROW], F32, name="s_h%d" % h)
+            for i in range(2):
+                nc.vector.tensor_copy(out=s_h[:, i, S : S + 1], in_=sink_raw[:, h : h + 1])
+            s_bufs.append(s_h)
+
+
+        prep_alloc(0)
+        for m in range(-1, N_UNITS + 5):
+            b, j = divmod(m, UNITS_PER_BATCH)
+            if valid(m) and j == 0 and b + 2 < B:
+                load(b + 2, False)
+            if valid(m) and j == 0 and b + 1 < B:
+                prep_alloc(b + 1)
+            exps(m - 1)
+            add_mask(m, 0)
+            add_mask(m, 1)
+            for c in FIRST_NEED.get(m + 1, ()):
+                words_transpose(0, c)
+                words_copy(0, c, c % 2 == 1)
+            qk(m + 1, 0)
+            pv(m - 5)
+            qk(m + 1, 1)
+            e_out_of_psum(m - 2)
+            e_transposes(m - 1)
+            finish(m - 5)
+            row_max(m)
+            if m == 1:
+                value_group(0, 0)
+                value_group(0, 1)
+                value_quant(0)
+            if valid(m) and j == 2:
+                value_group(b + 1, 0)
+            if valid(m) and j == 4:
+                value_group(b + 1, 1)
+            if valid(m) and j == 6:
+                value_quant(b + 1)
+            e_quant(m - 3)
+            recip(m - 2)
+            e_regroup(m - 2)
+            if valid(m - 1):
+                b1, j1 = divmod(m - 1, UNITS_PER_BATCH)
+                words_copy(b1 + 1, j1 - FIRST_GROUP_ROUND, False)
+            if valid(m):
+                words_transpose(b + 1, j - FIRST_GROUP_ROUND)

@@ -19,14 +19,18 @@ NT = S // P
 W = D // 2
 SCALE = 1.0 / 16.0
 ROW = 520
+EXT = S + 4
+FILL = -1.0e30
 UNITS_PER_BATCH = H * NT // 2
 N_UNITS = B * UNITS_PER_BATCH
 TILE_E = P * NT
+E_HALF = EXT // 2
 DEN_STEP = 8
-N_DIRECT = 2
 WORD_GROUPS = (("k", 0), ("q", 0), ("q", 1), ("k", 1), ("q", 2), ("q", 3))
 FIRST_NEED = {0: (0, 1), 1: (2,), 2: (3, 4), 3: (5,)}
+VECTOR_GROUPS = (1, 4)
 FIRST_GROUP_ROUND = 2
+V_PIECES = 8
 FLOPS = 2 * 2 * B * H * S * S * D
 
 
@@ -39,7 +43,6 @@ def tile_deepseekv4attention_t_kernel(tc, query, key, value, attention_mask, sin
         prep3 = ctx.enter_context(tc.tile_pool(name="prep3", bufs=3))
         work = ctx.enter_context(tc.tile_pool(name="work", bufs=3))
         work4 = ctx.enter_context(tc.tile_pool(name="work4", bufs=4))
-        one = ctx.enter_context(tc.tile_pool(name="one", bufs=1))
         stat = ctx.enter_context(tc.tile_pool(name="stat", bufs=6))
         outp = ctx.enter_context(tc.tile_pool(name="outp", bufs=3))
         ps_sc = ctx.enter_context(tc.psum_pool(name="ps_sc", bufs=4))
@@ -65,10 +68,7 @@ def tile_deepseekv4attention_t_kernel(tc, query, key, value, attention_mask, sin
             return j == UNITS_PER_BATCH - 1 or (j == 3 and b % 2 == 0)
 
         def mask_tile(b, t):
-            return loaded[b]["m"][:, t * S : (t + 1) * S].rearrange("p (w t) -> p t w", t=NT)
-
-        def direct(n):
-            return n >= N_UNITS - N_DIRECT
+            return loaded[b]["m"][:, t * S : (t + 1) * S]
 
 
         def load(b, fine):
@@ -141,18 +141,30 @@ def tile_deepseekv4attention_t_kernel(tc, query, key, value, attention_mask, sin
             which, blk = WORD_GROUPS[c]
             dst_cols = ready[b][which][:, blk * NT * P : (blk + 1) * NT * P]
             tq = st[(b, "tq", c)]
-            if on_vector:
-                nc.vector.tensor_copy(out=dst_cols, in_=tq[:].rearrange("p t q -> p (t q)"))
+            if which == "k":
+                dst = dst_cols.rearrange("p (r t) -> p r t", t=NT)
+                src = tq[:].rearrange("p t r -> p r t")
             else:
-                nc.scalar.copy(out=dst_cols, in_=tq[:].rearrange("p t q -> p (t q)"))
+                dst = dst_cols
+                src = tq[:].rearrange("p t r -> p (t r)")
+            if on_vector:
+                nc.vector.tensor_copy(out=dst, in_=src)
+            else:
+                nc.scalar.copy(out=dst, in_=src)
 
-        def value_group(b, g):
+        def value_piece(b, x):
             if b >= B:
                 return
-            cols = slice(g * D * NT, (g + 1) * D * NT)
-            nc.vector.tensor_copy(
-                out=ready[b]["vg"][:, cols].rearrange("p (c i t) -> p c t i", i=4, t=NT),
-                in_=loaded[b]["v"][:, cols].rearrange("p (t c i) -> p c t i", i=4, t=NT),
+            g, y = divmod(x, V_PIECES // HKV)
+            wd = D * HKV // V_PIECES
+            src = loaded[b]["v"][:, g * NT * D : (g + 1) * NT * D].rearrange("p (t d) -> p t d", t=NT)
+            nc.gpsimd.tensor_scalar(
+                out=ready[b]["vg"][:, x * wd * NT : (x + 1) * wd * NT].rearrange("p (c i t) -> p c t i", i=4, t=NT),
+                in0=src[:, :, y * wd : (y + 1) * wd].rearrange("p t (c i) -> p c t i", i=4),
+                scalar1=1.0,
+                scalar2=0.0,
+                op0=ALU.mult,
+                op1=ALU.add,
             )
 
         def value_quant(b):
@@ -175,7 +187,7 @@ def tile_deepseekv4attention_t_kernel(tc, query, key, value, attention_mask, sin
             on_pe = mask_on_pe(n)
             if on_pe:
                 nc.tensor.matmul(
-                    sc[:].rearrange("p (t w) -> p t w", t=NT), lhsT=ident16[:], rhs=mask_tile(b, t), start=True, stop=False
+                    sc[:], lhsT=ident16[:], rhs=mask_tile(b, t), start=True, stop=False
                 )
             for e in range(2):
                 nc.tensor.matmul(
@@ -201,8 +213,8 @@ def tile_deepseekv4attention_t_kernel(tc, query, key, value, attention_mask, sin
                 )
                 return
             nc.vector.scalar_tensor_tensor(
-                out=s_bufs[h][:, i, 0:S].rearrange("p (t w) -> p t w", t=NT),
-                in0=st[(n, "sc", i)][:].rearrange("p (t w) -> p t w", t=NT),
+                out=s_bufs[h][:, i, 0:S],
+                in0=st[(n, "sc", i)][:],
                 scalar=SCALE,
                 in1=mask_tile(b, t),
                 op0=ALU.mult,
@@ -234,7 +246,7 @@ def tile_deepseekv4attention_t_kernel(tc, query, key, value, attention_mask, sin
                 return
             b, tp, h = where(n)
             negm = st[(n, "negm")]
-            e_sb = work.tile([P, 2, ROW], BF16, tag="e_sb")
+            e_sb = work.tile([P, 2, 2, E_HALF], BF16, tag="e_sb")
             if n % 2 == 0:
                 den_pair = stat.tile([P, 2 * DEN_STEP], F32, tag="den_pair")
                 st[(n // 2, "den_pair")] = den_pair
@@ -246,8 +258,8 @@ def tile_deepseekv4attention_t_kernel(tc, query, key, value, attention_mask, sin
             for i in range(2):
                 if mask_on_pe(n):
                     nc.scalar.activation(
-                        out=e_sb[:, i, 0:S],
-                        in_=st[(n, "sc", i)][:],
+                        out=e_sb[:, i, :, 0 : S // 2].rearrange("p u (w v) -> p u w v", v=2),
+                        in_=st[(n, "sc", i)][:].rearrange("p (w u v) -> p u w v", u=2, v=2),
                         func=ACT.Exp,
                         bias=negm[:, i : i + 1],
                         scale=SCALE,
@@ -255,8 +267,8 @@ def tile_deepseekv4attention_t_kernel(tc, query, key, value, attention_mask, sin
                     )
                 else:
                     nc.scalar.activation(
-                        out=e_sb[:, i, 0 : S + 1],
-                        in_=s_bufs[h][:, i, 0 : S + 1],
+                        out=e_sb[:, i, :, :].rearrange("p u (w v) -> p u w v", v=2),
+                        in_=s_bufs[h][:, i, 0:EXT].rearrange("p (w u v) -> p u w v", u=2, v=2),
                         func=ACT.Exp,
                         bias=negm[:, i : i + 1],
                         scale=1.0,
@@ -287,58 +299,30 @@ def tile_deepseekv4attention_t_kernel(tc, query, key, value, attention_mask, sin
             if not valid(n):
                 return
             e_sb = st[(n, "e")]
-            et = ps_et.tile([P, 2, NT, P], BF16, tag="et")
+            et = ps_et.tile([P, 2, 2, P], F32, tag="et")
             for i in range(2):
-                for t in range(NT):
-                    nc.tensor.transpose(et[:, i, t, :], e_sb[:, i, t * P : (t + 1) * P], ident_b[:])
+                for u in range(2):
+                    nc.tensor.transpose(et[:, i, u, :], e_sb[:, i, u, 0 : S // 2].bitcast(F32), ident_f[:])
             st[(n, "et")] = et
 
         def e_out_of_psum(n):
             if not valid(n):
                 return
-            et = st[(n, "et")]
-            if direct(n):
-                gr_v = work.tile([P, 2 * TILE_E], BF16, tag="gr_v", align_bytes=64)
-                nc.vector.tensor_copy(
-                    out=gr_v[:].rearrange("p (i q t) -> p i q t", i=2, t=NT), in_=et[:].rearrange("p i t q -> p i q t")
-                )
-                st[(n, "gr")] = gr_v[:]
-                return
-            etc = work4.tile([P, 2 * TILE_E], BF16, tag="etc")
-            nc.scalar.copy(out=etc[:], in_=et[:].rearrange("p i t q -> p (i t q)"))
-            st[(n, "etc")] = etc
-
-        def e_regroup(n):
-            if not valid(n) or direct(n):
-                return
-            if n % 2 == 0:
-                gr = one.tile([P, 4 * TILE_E], BF16, tag="gr", align_bytes=64)
-                st[(n // 2, "gr_pair")] = gr
-            half = st[(n // 2, "gr_pair")][:, (n % 2) * 2 * TILE_E : (n % 2 + 1) * 2 * TILE_E]
-            nc.gpsimd.tensor_scalar(
-                out=half.rearrange("p (i q t) -> p i q t", i=2, t=NT),
-                in0=st[(n, "etc")][:].rearrange("p (i t q) -> p i q t", i=2, t=NT),
-                scalar1=1.0,
-                scalar2=0.0,
-                op0=ALU.mult,
-                op1=ALU.add,
+            gr = work4.tile([P, 2 * TILE_E], BF16, tag="gr", align_bytes=64)
+            nc.scalar.copy(
+                out=gr[:].bitcast(F32).rearrange("p (i q u) -> p i q u", i=2, u=2),
+                in_=st[(n, "et")][:].rearrange("p i u q -> p i q u"),
             )
+            st[(n, "gr")] = gr
 
         def e_quant(n):
             if not valid(n):
                 return
-            if n % 2 == 0:
-                ec = work.tile([P, 4 * P], U32, tag="ec", align_bytes=64)
-                es = work.tile([P, 4 * P], U8, tag="es", align_bytes=64)
-                st[(n // 2, "ec")] = ec
-                st[(n // 2, "es")] = es
-            ec = st[(n // 2, "ec")]
-            es = st[(n // 2, "es")]
-            if direct(n):
-                cols = slice((n % 2) * 2 * P, (n % 2 + 1) * 2 * P)
-                nc.vector.quantize_mx(out=ec[:, cols].bitcast(FP8X4), scales=es[:, cols], in_=st[(n, "gr")])
-            elif n % 2 == 1:
-                nc.vector.quantize_mx(out=ec[:].bitcast(FP8X4), scales=es[:], in_=st[(n // 2, "gr_pair")][:])
+            ec = work.tile([P, 2 * P], U32, tag="ec", align_bytes=64)
+            es = work.tile([P, 2 * P], U8, tag="es", align_bytes=64)
+            nc.vector.quantize_mx(out=ec[:].bitcast(FP8X4), scales=es[:], in_=st[(n, "gr")][:])
+            st[(n, "ec")] = ec
+            st[(n, "es")] = es
 
         def pv(n):
             if not valid(n):
@@ -347,11 +331,11 @@ def tile_deepseekv4attention_t_kernel(tc, query, key, value, attention_mask, sin
             g = h // G
             vc = ready[b]["vc"]
             vs = ready[b]["vs"]
-            ec = st[(n // 2, "ec")]
-            es = st[(n // 2, "es")]
+            ec = st[(n, "ec")]
+            es = st[(n, "es")]
             o_ps = ps_o.tile([P, 2, D], F32, tag="o_ps")
             for i in range(2):
-                cols = slice(((n % 2) * 2 + i) * P, ((n % 2) * 2 + i + 1) * P)
+                cols = slice(i * P, (i + 1) * P)
                 nc.tensor.matmul_mx(
                     out=o_ps[:, i, :],
                     lhsT=ec[:, cols].bitcast(FP8X4),
@@ -405,12 +389,13 @@ def tile_deepseekv4attention_t_kernel(tc, query, key, value, attention_mask, sin
         for h in range(H):
             s_h = const.tile([P, 2, ROW], F32, name="s_h%d" % h)
             for i in range(2):
+                nc.vector.memset(s_h[:, i, S:ROW], FILL)
                 nc.vector.tensor_copy(out=s_h[:, i, S : S + 1], in_=sink_raw[:, h : h + 1])
             s_bufs.append(s_h)
 
 
         prep_alloc(0)
-        for m in range(-1, N_UNITS + 5):
+        for m in range(-1, N_UNITS + 4):
             b, j = divmod(m, UNITS_PER_BATCH)
             if valid(m) and j == 0 and b + 2 < B:
                 load(b + 2, False)
@@ -423,27 +408,26 @@ def tile_deepseekv4attention_t_kernel(tc, query, key, value, attention_mask, sin
                 words_transpose(0, c)
                 words_copy(0, c, c % 2 == 1)
             qk(m + 1, 0)
-            pv(m - 5)
+            pv(m - 4)
             qk(m + 1, 1)
             e_out_of_psum(m - 2)
             e_transposes(m - 1)
-            finish(m - 5)
+            finish(m - 4)
             row_max(m)
+            if m == 0:
+                for x in range(V_PIECES):
+                    value_piece(0, x)
             if m == 1:
-                value_group(0, 0)
-                value_group(0, 1)
                 value_quant(0)
-            if valid(m) and j == 2:
-                value_group(b + 1, 0)
-            if valid(m) and j == 4:
-                value_group(b + 1, 1)
-            if valid(m) and j == 6:
-                value_quant(b + 1)
-            e_quant(m - 3)
+            if valid(m):
+                value_piece(b + 1, j)
+                if j == 0 and b > 0:
+                    value_quant(b)
+            e_quant(m - 2)
             recip(m - 2)
-            e_regroup(m - 2)
             if valid(m - 1):
                 b1, j1 = divmod(m - 1, UNITS_PER_BATCH)
-                words_copy(b1 + 1, j1 - FIRST_GROUP_ROUND, False)
+                c1 = j1 - FIRST_GROUP_ROUND
+                words_copy(b1 + 1, c1, c1 in VECTOR_GROUPS)
             if valid(m):
                 words_transpose(b + 1, j - FIRST_GROUP_ROUND)

@@ -30,7 +30,6 @@ WORD_GROUPS = (("k", 0), ("q", 0), ("q", 1), ("k", 1), ("q", 2), ("q", 3))
 FIRST_NEED = {0: (0, 1), 1: (2,), 2: (3, 4), 3: (5,)}
 VECTOR_GROUPS = (1, 4)
 FIRST_GROUP_ROUND = 2
-V_PIECES = 8
 FLOPS = 2 * 2 * B * H * S * S * D
 
 
@@ -152,19 +151,13 @@ def tile_deepseekv4attention_t_kernel(tc, query, key, value, attention_mask, sin
             else:
                 nc.scalar.copy(out=dst, in_=src)
 
-        def value_piece(b, x):
+        def value_group(b, g):
             if b >= B:
                 return
-            g, y = divmod(x, V_PIECES // HKV)
-            wd = D * HKV // V_PIECES
-            src = loaded[b]["v"][:, g * NT * D : (g + 1) * NT * D].rearrange("p (t d) -> p t d", t=NT)
-            nc.gpsimd.tensor_scalar(
-                out=ready[b]["vg"][:, x * wd * NT : (x + 1) * wd * NT].rearrange("p (c i t) -> p c t i", i=4, t=NT),
-                in0=src[:, :, y * wd : (y + 1) * wd].rearrange("p t (c i) -> p c t i", i=4),
-                scalar1=1.0,
-                scalar2=0.0,
-                op0=ALU.mult,
-                op1=ALU.add,
+            cols = slice(g * D * NT, (g + 1) * D * NT)
+            nc.vector.tensor_copy(
+                out=ready[b]["vg"][:, cols].rearrange("p (c i t) -> p c t i", i=4, t=NT),
+                in_=loaded[b]["v"][:, cols].rearrange("p (t c i) -> p c t i", i=4, t=NT),
             )
 
         def value_quant(b):
@@ -413,21 +406,22 @@ def tile_deepseekv4attention_t_kernel(tc, query, key, value, attention_mask, sin
             e_out_of_psum(m - 2)
             e_transposes(m - 1)
             finish(m - 4)
-            row_max(m)
-            if m == 0:
-                for x in range(V_PIECES):
-                    value_piece(0, x)
             if m == 1:
+                value_group(0, 0)
+                value_group(0, 1)
                 value_quant(0)
-            if valid(m):
-                value_piece(b + 1, j)
-                if j == 0 and b > 0:
-                    value_quant(b)
-            e_quant(m - 2)
+            if valid(m) and j == 2:
+                value_group(b + 1, 0)
+            if valid(m) and j == 4:
+                value_group(b + 1, 1)
+            if valid(m) and j == 6:
+                value_quant(b + 1)
+            e_quant(m - 3)
             recip(m - 2)
             if valid(m - 1):
                 b1, j1 = divmod(m - 1, UNITS_PER_BATCH)
                 c1 = j1 - FIRST_GROUP_ROUND
                 words_copy(b1 + 1, c1, c1 in VECTOR_GROUPS)
+            row_max(m)
             if valid(m):
                 words_transpose(b + 1, j - FIRST_GROUP_ROUND)

@@ -30,6 +30,7 @@ WORD_GROUPS = (("k", 0), ("q", 0), ("q", 1), ("k", 1), ("q", 2), ("q", 3))
 FIRST_NEED = {0: (0, 1), 1: (2,), 2: (3, 4), 3: (5,)}
 VECTOR_GROUPS = (1, 4)
 FIRST_GROUP_ROUND = 2
+V_PIECES = 8
 FLOPS = 2 * 2 * B * H * S * S * D
 
 
@@ -151,13 +152,19 @@ def tile_deepseekv4attention_t_kernel(tc, query, key, value, attention_mask, sin
             else:
                 nc.scalar.copy(out=dst, in_=src)
 
-        def value_group(b, g):
+        def value_piece(b, x):
             if b >= B:
                 return
-            cols = slice(g * D * NT, (g + 1) * D * NT)
-            nc.vector.tensor_copy(
-                out=ready[b]["vg"][:, cols].rearrange("p (c i t) -> p c t i", i=4, t=NT),
-                in_=loaded[b]["v"][:, cols].rearrange("p (t c i) -> p c t i", i=4, t=NT),
+            g, y = divmod(x, V_PIECES // HKV)
+            wd = D * HKV // V_PIECES
+            src = loaded[b]["v"][:, g * NT * D : (g + 1) * NT * D].rearrange("p (t d) -> p t d", t=NT)
+            nc.gpsimd.tensor_scalar(
+                out=ready[b]["vg"][:, x * wd * NT : (x + 1) * wd * NT].rearrange("p (d t) -> p d t", t=NT),
+                in0=src[:, :, y * wd : (y + 1) * wd].rearrange("p t d -> p d t"),
+                scalar1=1.0,
+                scalar2=0.0,
+                op0=ALU.mult,
+                op1=ALU.add,
             )
 
         def value_quant(b):
@@ -388,6 +395,8 @@ def tile_deepseekv4attention_t_kernel(tc, query, key, value, attention_mask, sin
 
 
         prep_alloc(0)
+        for x in range(V_PIECES):
+            value_piece(0, x)
         for m in range(-1, N_UNITS + 4):
             b, j = divmod(m, UNITS_PER_BATCH)
             if valid(m) and j == 0 and b + 2 < B:
@@ -403,19 +412,15 @@ def tile_deepseekv4attention_t_kernel(tc, query, key, value, attention_mask, sin
             qk(m + 1, 0)
             pv(m - 4)
             qk(m + 1, 1)
+            if valid(m):
+                value_piece(b + 1, j)
             e_out_of_psum(m - 2)
             e_transposes(m - 1)
             finish(m - 4)
             if m == 1:
-                value_group(0, 0)
-                value_group(0, 1)
                 value_quant(0)
-            if valid(m) and j == 2:
-                value_group(b + 1, 0)
-            if valid(m) and j == 4:
-                value_group(b + 1, 1)
-            if valid(m) and j == 6:
-                value_quant(b + 1)
+            if valid(m) and j == 0 and b > 0:
+                value_quant(b)
             e_quant(m - 3)
             recip(m - 2)
             if valid(m - 1):

@@ -27,10 +27,11 @@ TILE_E = P * NT
 E_HALF = EXT // 2
 DEN_STEP = 8
 WORD_GROUPS = (("k", 0), ("q", 0), ("q", 1), ("k", 1), ("q", 2), ("q", 3))
-FIRST_NEED = {0: (0, 1), 1: (2,), 2: (3, 4), 3: (5,)}
+FIRST_NEED = {0: (0, 1), 1: (2, 3, 4, 5)}
 VECTOR_GROUPS = (1, 4)
 FIRST_GROUP_ROUND = 2
 V_PIECES = 8
+N_LATE = 4
 FLOPS = 2 * 2 * B * H * S * S * D
 
 
@@ -69,6 +70,9 @@ def tile_deepseekv4attention_t_kernel(tc, query, key, value, attention_mask, sin
 
         def mask_tile(b, t):
             return loaded[b]["m"][:, t * S : (t + 1) * S]
+
+        def late(n):
+            return n >= N_UNITS - N_LATE
 
 
         def load(b, fine):
@@ -129,7 +133,11 @@ def tile_deepseekv4attention_t_kernel(tc, query, key, value, attention_mask, sin
                 return
             which, blk = WORD_GROUPS[c]
             src = loaded[b][which]
-            tq = ps_tq.tile([P, NT, P], F32, tag="tq")
+            if b == 0:
+                pool, tag = ((ps_tq, "tq"), (ps_et, "et"), (ps_o, "o_ps"))[c % 3]
+                tq = pool.tile([P, NT, P], F32, tag=tag)
+            else:
+                tq = ps_tq.tile([P, NT, P], F32, tag="tq")
             for t in range(NT):
                 c0 = (blk * NT + t) * W
                 nc.tensor.transpose(tq[:, t, :], src[:].bitcast(F32)[:, c0 : c0 + W], ident_f[:])
@@ -152,11 +160,14 @@ def tile_deepseekv4attention_t_kernel(tc, query, key, value, attention_mask, sin
             else:
                 nc.scalar.copy(out=dst, in_=src)
 
-        def value_piece(b, x):
+        def value_piece(b, x, pace):
             if b >= B:
                 return
             g, y = divmod(x, V_PIECES // HKV)
             wd = D * HKV // V_PIECES
+            if pace is not None:
+                seen = stat.tile([P, 2], F32, tag="seen")
+                nc.gpsimd.tensor_scalar(out=seen[:], in0=pace, scalar1=1.0, scalar2=0.0, op0=ALU.mult, op1=ALU.add)
             src = loaded[b]["v"][:, g * NT * D : (g + 1) * NT * D].rearrange("p (t d) -> p t d", t=NT)
             nc.gpsimd.tensor_scalar(
                 out=ready[b]["vg"][:, x * wd * NT : (x + 1) * wd * NT].rearrange("p (d t) -> p d t", t=NT),
@@ -333,7 +344,10 @@ def tile_deepseekv4attention_t_kernel(tc, query, key, value, attention_mask, sin
             vs = ready[b]["vs"]
             ec = st[(n, "ec")]
             es = st[(n, "es")]
-            o_ps = ps_o.tile([P, 2, D], F32, tag="o_ps")
+            if late(n):
+                o_ps = ps_sc.tile([P, 2, D], F32, tag="sc")
+            else:
+                o_ps = ps_o.tile([P, 2, D], F32, tag="o_ps")
             for i in range(2):
                 cols = slice(i * P, (i + 1) * P)
                 nc.tensor.matmul_mx(
@@ -358,7 +372,14 @@ def tile_deepseekv4attention_t_kernel(tc, query, key, value, attention_mask, sin
                 st[(b, tp, "o_sb")] = o_new
             o_sb = st[(b, tp, "o_sb")]
             for i in range(2):
-                nc.scalar.activation(out=o_sb[:, i, h, :], in_=o_ps[:, i, :], func=ACT.Copy, scale=rden[:, i : i + 1])
+                if late(n) and (i == 0 or n < N_UNITS - 1):
+                    nc.vector.tensor_scalar(
+                        out=o_sb[:, i, h, :], in0=o_ps[:, i, :], scalar1=rden[:, i : i + 1], scalar2=None, op0=ALU.mult
+                    )
+                else:
+                    nc.scalar.activation(
+                        out=o_sb[:, i, h, :], in_=o_ps[:, i, :], func=ACT.Copy, scale=rden[:, i : i + 1]
+                    )
             if b == B - 1 and tp == 1:
                 nc.sync.dma_start(
                     out=out[b].rearrange("(p t) h d -> p t h d", t=NT)[:, 2 * tp : 2 * tp + 2, h, :],
@@ -396,7 +417,7 @@ def tile_deepseekv4attention_t_kernel(tc, query, key, value, attention_mask, sin
 
         prep_alloc(0)
         for x in range(V_PIECES):
-            value_piece(0, x)
+            value_piece(0, x, None)
         for m in range(-1, N_UNITS + 4):
             b, j = divmod(m, UNITS_PER_BATCH)
             if valid(m) and j == 0 and b + 2 < B:
@@ -408,16 +429,16 @@ def tile_deepseekv4attention_t_kernel(tc, query, key, value, attention_mask, sin
             add_mask(m, 1)
             for c in FIRST_NEED.get(m + 1, ()):
                 words_transpose(0, c)
-                words_copy(0, c, c % 2 == 1)
+                words_copy(0, c, c == 1)
             qk(m + 1, 0)
             pv(m - 4)
             qk(m + 1, 1)
             if valid(m):
-                value_piece(b + 1, j)
+                value_piece(b + 1, j, st[(m - 1, "negm")][:] if valid(m - 1) else None)
             e_out_of_psum(m - 2)
             e_transposes(m - 1)
             finish(m - 4)
-            if m == 1:
+            if m == 2:
                 value_quant(0)
             if valid(m) and j == 0 and b > 0:
                 value_quant(b)

@@ -427,6 +427,10 @@ def tile_deepseekv4attention_t_kernel(tc, query, key, value, attention_mask, sin
             exps(m - 1)
             add_mask(m, 0)
             add_mask(m, 1)
+            if valid(m - 1):
+                b1, j1 = divmod(m - 1, UNITS_PER_BATCH)
+                c1 = j1 - FIRST_GROUP_ROUND
+                words_copy(b1 + 1, c1, c1 in VECTOR_GROUPS)
             for c in FIRST_NEED.get(m + 1, ()):
                 words_transpose(0, c)
                 words_copy(0, c, c == 1)
@@ -444,10 +448,6 @@ def tile_deepseekv4attention_t_kernel(tc, query, key, value, attention_mask, sin
                 value_quant(b)
             e_quant(m - 3)
             recip(m - 2)
-            if valid(m - 1):
-                b1, j1 = divmod(m - 1, UNITS_PER_BATCH)
-                c1 = j1 - FIRST_GROUP_ROUND
-                words_copy(b1 + 1, c1, c1 in VECTOR_GROUPS)
             row_max(m)
             if valid(m):
                 words_transpose(b + 1, j - FIRST_GROUP_ROUND)

@@ -26,12 +26,23 @@ N_UNITS = B * UNITS_PER_BATCH
 TILE_E = P * NT
 E_HALF = EXT // 2
 DEN_STEP = 8
-WORD_GROUPS = (("k", 0), ("q", 0), ("q", 1), ("k", 1), ("q", 2), ("q", 3))
-FIRST_NEED = {0: (0, 1), 1: (2, 3, 4, 5)}
-VECTOR_GROUPS = (1, 4)
-FIRST_GROUP_ROUND = 2
+PIECES = (("k", 0, 1, 0, 4), ("q", 0, 1, 0, 4), ("q", 1, 1, 0, 4), ("k", 1, 1, 0, 4), ("q", 2, 1, 0, 4), ("q", 3, 1, 0, 4))
+VECTOR_PIECES = (1, 4)
+FIRST_PIECES = (
+    ("k", 0, 1, 0, 4),
+    ("q", 0, 1, 0, 2),
+    ("q", 1, 1, 0, 2),
+    ("k", 1, 1, 0, 4),
+    ("q", 2, 2, 0, 2),
+    ("q", 0, 2, 2, 2),
+    ("q", 2, 2, 2, 2),
+)
+FIRST_NEED = {0: (0, 1), 1: (2, 3, 4), 2: (5,), 3: (6,)}
+FIRST_BY_VECTOR = (1, 2)
+FIRST_PIECE_ROUND = 2
 V_PIECES = 8
-N_LATE = 4
+N_LATE = 7
+PE_UNITS = (1, 4, 7)
 FLOPS = 2 * 2 * B * H * S * S * D
 
 
@@ -64,9 +75,8 @@ def tile_deepseekv4attention_t_kernel(tc, query, key, value, attention_mask, sin
             tp, h = divmod(j, H)
             return b, tp, h
 
-        def mask_on_pe(n):
-            b, j = divmod(n, UNITS_PER_BATCH)
-            return j == UNITS_PER_BATCH - 1 or (j == 3 and b % 2 == 0)
+        def mask_on_pe(n, i):
+            return i == 1 and n % UNITS_PER_BATCH in PE_UNITS or n == N_UNITS - 1
 
         def mask_tile(b, t):
             return loaded[b]["m"][:, t * S : (t + 1) * S]
@@ -89,10 +99,10 @@ def tile_deepseekv4attention_t_kernel(tc, query, key, value, attention_mask, sin
                     in_=key[b, g0:g1].rearrange("g (p t) d -> p g (t d)", t=NT),
                 )
 
-            def load_q(h0, h1):
+            def load_q(tp, h0, h1):
                 nc.sync.dma_start(
-                    out=q_sb[:, h0 * blk : h1 * blk].rearrange("p (h x) -> p h x", x=blk),
-                    in_=query[b, h0:h1].rearrange("h (p t) d -> p h (t d)", t=NT),
+                    out=q_sb[:].rearrange("p (a x) -> p a x", x=2 * D)[:, tp * H + h0 : tp * H + h1, :],
+                    in_=query[b, h0:h1].rearrange("h (p t) d -> p h (t d)", t=NT)[:, :, tp * 2 * D : (tp + 1) * 2 * D],
                 )
 
             def load_m(t0, t1):
@@ -103,16 +113,17 @@ def tile_deepseekv4attention_t_kernel(tc, query, key, value, attention_mask, sin
 
             if fine:
                 load_k(0, 1)
-                load_q(0, 1)
+                load_q(0, 0, 1)
+                load_q(0, 1, 2)
                 load_m(0, 2)
-                load_q(1, 2)
                 load_k(1, 2)
-                load_q(2, 3)
-                load_q(3, 4)
+                load_q(0, 2, H)
+                load_q(1, 0, H)
                 load_m(2, NT)
             else:
                 load_k(0, HKV)
-                load_q(0, H)
+                load_q(0, 0, H)
+                load_q(1, 0, H)
                 load_m(0, NT)
             nc.sync.dma_start(
                 out=v_sb[:].rearrange("p (g x) -> p g x", x=blk),
@@ -128,33 +139,32 @@ def tile_deepseekv4attention_t_kernel(tc, query, key, value, attention_mask, sin
             vs = prep3.tile([P, HKV * D], U8, tag="vs", align_bytes=64)
             ready[b] = {"q": qT, "k": kT, "vg": vg, "vc": vc, "vs": vs}
 
-        def words_transpose(b, c):
-            if b >= B or not 0 <= c < len(WORD_GROUPS):
-                return
-            which, blk = WORD_GROUPS[c]
+        def words_transpose(b, piece):
+            which, h0, nh, t0, nt = piece
             src = loaded[b][which]
             if b == 0:
-                pool, tag = ((ps_tq, "tq"), (ps_et, "et"), (ps_o, "o_ps"))[c % 3]
+                pool, tag = ((ps_tq, "tq"), (ps_et, "et"), (ps_o, "o_ps"))[FIRST_PIECES.index(piece) % 3]
                 tq = pool.tile([P, NT, P], F32, tag=tag)
             else:
                 tq = ps_tq.tile([P, NT, P], F32, tag="tq")
-            for t in range(NT):
-                c0 = (blk * NT + t) * W
-                nc.tensor.transpose(tq[:, t, :], src[:].bitcast(F32)[:, c0 : c0 + W], ident_f[:])
-            st[(b, "tq", c)] = tq
+            for x in range(nh * nt):
+                hx, tx = h0 + x // nt, t0 + x % nt
+                if which == "k":
+                    c0 = (hx * NT + tx) * W
+                else:
+                    c0 = ((tx // 2 * H + hx) * 2 + tx % 2) * W
+                nc.tensor.transpose(tq[:, x, :], src[:].bitcast(F32)[:, c0 : c0 + W], ident_f[:])
+            st[(b, "tq", piece)] = tq
 
-        def words_copy(b, c, on_vector):
-            if b >= B or not 0 <= c < len(WORD_GROUPS):
-                return
-            which, blk = WORD_GROUPS[c]
-            dst_cols = ready[b][which][:, blk * NT * P : (blk + 1) * NT * P]
-            tq = st[(b, "tq", c)]
+        def words_copy(b, piece, on_vector):
+            which, h0, nh, t0, nt = piece
+            tq = st[(b, "tq", piece)]
             if which == "k":
-                dst = dst_cols.rearrange("p (r t) -> p r t", t=NT)
+                dst = ready[b]["k"][:, h0 * S : (h0 + 1) * S].rearrange("p (r t) -> p r t", t=NT)
                 src = tq[:].rearrange("p t r -> p r t")
             else:
-                dst = dst_cols
-                src = tq[:].rearrange("p t r -> p (t r)")
+                dst = ready[b]["q"][:].rearrange("p (h x) -> p h x", h=H)[:, h0 : h0 + nh, t0 * P : (t0 + nt) * P]
+                src = tq[:, 0 : nh * nt, :].rearrange("p (h t) r -> p h (t r)", h=nh)
             if on_vector:
                 nc.vector.tensor_copy(out=dst, in_=src)
             else:
@@ -195,7 +205,7 @@ def tile_deepseekv4attention_t_kernel(tc, query, key, value, attention_mask, sin
             kTb = ready[b]["k"][:].bitcast(BF16).rearrange("p (c e) -> p c e", e=2)
             sc = ps_sc.tile([P, S], F32, tag="sc")
             c0 = (h * NT + t) * P
-            on_pe = mask_on_pe(n)
+            on_pe = mask_on_pe(n, i)
             if on_pe:
                 nc.tensor.matmul(
                     sc[:], lhsT=ident16[:], rhs=mask_tile(b, t), start=True, stop=False
@@ -215,16 +225,23 @@ def tile_deepseekv4attention_t_kernel(tc, query, key, value, attention_mask, sin
                 return
             b, tp, h = where(n)
             t = 2 * tp + i
-            if mask_on_pe(n):
-                if i == 0:
-                    nm16 = stat.tile([P, 2], F32, tag="nm16")
-                    st[(n, "nm16")] = nm16
-                nc.vector.tensor_reduce(
-                    out=st[(n, "nm16")][:, i : i + 1], in_=st[(n, "sc", i)][:], axis=AX.X, op=ALU.max, negate=True
+            if i == 0:
+                negm = stat.tile([P, 2], F32, tag="negm")
+                st[(n, "negm")] = negm
+            if mask_on_pe(n, i):
+                minus_s = work.tile([P, S], BF16, tag="minus_s")
+                nc.vector.tensor_scalar(
+                    out=minus_s[:],
+                    in0=st[(n, "sc", i)][:],
+                    scalar1=-SCALE,
+                    scalar2=nsink[:, h : h + 1],
+                    op0=ALU.mult,
+                    op1=ALU.min,
+                    accum_out=st[(n, "negm")][:, i : i + 1],
                 )
                 return
             nc.vector.scalar_tensor_tensor(
-                out=s_bufs[h][:, i, 0:S],
+                out=s_all[:, h, i, 0:S],
                 in0=st[(n, "sc", i)][:],
                 scalar=SCALE,
                 in1=mask_tile(b, t),
@@ -236,21 +253,11 @@ def tile_deepseekv4attention_t_kernel(tc, query, key, value, attention_mask, sin
             if not valid(n):
                 return
             b, tp, h = where(n)
-            negm = stat.tile([P, 2], F32, tag="negm")
-            if mask_on_pe(n):
-                nc.vector.tensor_scalar(
-                    out=negm[:],
-                    in0=st[(n, "nm16")][:],
-                    scalar1=SCALE,
-                    scalar2=nsink[:, h : h + 1],
-                    op0=ALU.mult,
-                    op1=ALU.min,
-                )
-            else:
+            k = sum(not mask_on_pe(n, i) for i in range(2))
+            if k > 0:
                 nc.vector.tensor_reduce(
-                    out=negm[:], in_=s_bufs[h][:, :, 0 : S + 1], axis=AX.X, op=ALU.max, negate=True
+                    out=st[(n, "negm")][:, 0:k], in_=s_all[:, h, 0:k, 0 : S + 1], axis=AX.X, op=ALU.max, negate=True
                 )
-            st[(n, "negm")] = negm
 
         def exps(n):
             if not valid(n):
@@ -262,76 +269,87 @@ def tile_deepseekv4attention_t_kernel(tc, query, key, value, attention_mask, sin
                 den_pair = stat.tile([P, 2 * DEN_STEP], F32, tag="den_pair")
                 st[(n // 2, "den_pair")] = den_pair
             c_den = (n % 2) * DEN_STEP
-            if mask_on_pe(n):
-                den = stat.tile([P, 2], F32, tag="den")
-            else:
-                den = st[(n // 2, "den_pair")][:, c_den : c_den + 2]
-            for i in range(2):
-                if mask_on_pe(n):
+            den = st[(n // 2, "den_pair")][:, c_den : c_den + 2]
+            for i in (1, 0) if mask_on_pe(n, 1) and not mask_on_pe(n, 0) else (0, 1):
+                if mask_on_pe(n, i):
+                    e_sum = stat.tile([P, 1], F32, tag="e_sum")
                     nc.scalar.activation(
                         out=e_sb[:, i, :, 0 : S // 2].rearrange("p u (w v) -> p u w v", v=2),
                         in_=st[(n, "sc", i)][:].rearrange("p (w u v) -> p u w v", u=2, v=2),
                         func=ACT.Exp,
                         bias=negm[:, i : i + 1],
                         scale=SCALE,
-                        accum_out=den[:, i : i + 1],
+                        accum_out=e_sum[:],
                     )
+                    e_sink = stat.tile([P, 1], F32, tag="e_sink")
+                    nc.scalar.activation(
+                        out=e_sink[:], in_=negm[:, i : i + 1], func=ACT.Exp, bias=sink_f[:, h : h + 1], scale=1.0
+                    )
+                    nc.gpsimd.tensor_tensor(out=den[:, i : i + 1], in0=e_sum[:], in1=e_sink[:], op=ALU.add)
                 else:
                     nc.scalar.activation(
                         out=e_sb[:, i, :, :].rearrange("p u (w v) -> p u w v", v=2),
-                        in_=s_bufs[h][:, i, 0:EXT].rearrange("p (w u v) -> p u w v", u=2, v=2),
+                        in_=s_all[:, h, i, 0:EXT].rearrange("p (w u v) -> p u w v", u=2, v=2),
                         func=ACT.Exp,
                         bias=negm[:, i : i + 1],
                         scale=1.0,
                         accum_out=den[:, i : i + 1],
                     )
-            if mask_on_pe(n):
-                sterm = stat.tile([P, 2], F32, tag="sterm")
-                nc.scalar.activation(out=sterm[:], in_=negm[:], func=ACT.Exp, bias=sink_f[:, h : h + 1], scale=1.0)
-                st[(n, "sterm")] = sterm
             st[(n, "e")] = e_sb
-            st[(n, "den")] = den
 
         def recip(n):
             if not valid(n):
                 return
             den_pair = st[(n // 2, "den_pair")]
-            c_den = (n % 2) * DEN_STEP
-            if mask_on_pe(n):
-                nc.vector.tensor_tensor(
-                    out=den_pair[:, c_den : c_den + 2], in0=st[(n, "den")][:], in1=st[(n, "sterm")][:], op=ALU.add
-                )
             if n % 2 == 1:
                 rden = stat.tile([P, 2, 2], F32, tag="rden")
                 nc.vector.reciprocal(out=rden[:], in_=den_pair[:].rearrange("p (a x) -> p a x", x=DEN_STEP)[:, :, 0:2])
                 st[(n // 2, "rden")] = rden
 
+        def parts(n):
+            return ((0,), (1,)) if n == N_UNITS - 1 else ((0, 1),)
+
         def e_transposes(n):
             if not valid(n):
                 return
             e_sb = st[(n, "e")]
-            et = ps_et.tile([P, 2, 2, P], F32, tag="et")
-            for i in range(2):
-                for u in range(2):
-                    nc.tensor.transpose(et[:, i, u, :], e_sb[:, i, u, 0 : S // 2].bitcast(F32), ident_f[:])
-            st[(n, "et")] = et
+            for part in parts(n):
+                et = ps_et.tile([P, 2, 2, P], F32, tag="et")
+                for x, i in enumerate(part):
+                    for u in range(2):
+                        nc.tensor.transpose(et[:, x, u, :], e_sb[:, i, u, 0 : S // 2].bitcast(F32), ident_f[:])
+                st[(n, "et", part)] = et
 
         def e_out_of_psum(n):
             if not valid(n):
                 return
             gr = work4.tile([P, 2 * TILE_E], BF16, tag="gr", align_bytes=64)
-            nc.scalar.copy(
-                out=gr[:].bitcast(F32).rearrange("p (i q u) -> p i q u", i=2, u=2),
-                in_=st[(n, "et")][:].rearrange("p i u q -> p i q u"),
-            )
             st[(n, "gr")] = gr
+            for part in parts(n):
+                k = len(part)
+                out_words = (
+                    gr[:, part[0] * TILE_E : (part[-1] + 1) * TILE_E]
+                    .bitcast(F32)
+                    .rearrange("p (i q u) -> p i q u", i=k, u=2)
+                )
+                in_words = st[(n, "et", part)][:, 0:k].rearrange("p i u q -> p i q u")
+                if n >= N_UNITS - 2 and part[0] == 0:
+                    nc.vector.tensor_copy(out=out_words, in_=in_words)
+                else:
+                    nc.scalar.copy(out=out_words, in_=in_words)
 
         def e_quant(n):
             if not valid(n):
                 return
             ec = work.tile([P, 2 * P], U32, tag="ec", align_bytes=64)
             es = work.tile([P, 2 * P], U8, tag="es", align_bytes=64)
-            nc.vector.quantize_mx(out=ec[:].bitcast(FP8X4), scales=es[:], in_=st[(n, "gr")][:])
+            for part in parts(n):
+                cols = slice(part[0] * P, (part[-1] + 1) * P)
+                nc.vector.quantize_mx(
+                    out=ec[:, cols].bitcast(FP8X4),
+                    scales=es[:, cols],
+                    in_=st[(n, "gr")][:, part[0] * TILE_E : (part[-1] + 1) * TILE_E],
+                )
             st[(n, "ec")] = ec
             st[(n, "es")] = es
 
@@ -344,42 +362,41 @@ def tile_deepseekv4attention_t_kernel(tc, query, key, value, attention_mask, sin
             vs = ready[b]["vs"]
             ec = st[(n, "ec")]
             es = st[(n, "es")]
-            if late(n):
-                o_ps = ps_sc.tile([P, 2, D], F32, tag="sc")
-            else:
-                o_ps = ps_o.tile([P, 2, D], F32, tag="o_ps")
-            for i in range(2):
-                cols = slice(i * P, (i + 1) * P)
-                nc.tensor.matmul_mx(
-                    out=o_ps[:, i, :],
-                    lhsT=ec[:, cols].bitcast(FP8X4),
-                    lhsT_scale=es[:, cols],
-                    rhs=vc[:, g * D : (g + 1) * D].bitcast(FP8X4),
-                    rhs_scale=vs[:, g * D : (g + 1) * D],
-                    start=True,
-                    stop=True,
-                )
-            st[(n, "o")] = o_ps
+            for part in parts(n):
+                if late(n):
+                    o_ps = ps_sc.tile([P, 2, D], F32, tag="sc")
+                else:
+                    o_ps = ps_o.tile([P, 2, D], F32, tag="o_ps")
+                for x, i in enumerate(part):
+                    cols = slice(i * P, (i + 1) * P)
+                    nc.tensor.matmul_mx(
+                        out=o_ps[:, x, :],
+                        lhsT=ec[:, cols].bitcast(FP8X4),
+                        lhsT_scale=es[:, cols],
+                        rhs=vc[:, g * D : (g + 1) * D].bitcast(FP8X4),
+                        rhs_scale=vs[:, g * D : (g + 1) * D],
+                        start=True,
+                        stop=True,
+                    )
+                    st[(n, "o", i)] = o_ps[:, x, :]
 
         def finish(n):
             if not valid(n):
                 return
             b, tp, h = where(n)
-            o_ps = st[(n, "o")]
             rden = st[(n // 2, "rden")][:, n % 2, :]
             if h == 0:
                 o_new = outp.tile([P, 2, H, D], F32, tag="o_sb")
                 st[(b, tp, "o_sb")] = o_new
             o_sb = st[(b, tp, "o_sb")]
             for i in range(2):
+                o_in = st[(n, "o", i)]
                 if late(n) and (i == 0 or n < N_UNITS - 1):
                     nc.vector.tensor_scalar(
-                        out=o_sb[:, i, h, :], in0=o_ps[:, i, :], scalar1=rden[:, i : i + 1], scalar2=None, op0=ALU.mult
+                        out=o_sb[:, i, h, :], in0=o_in, scalar1=rden[:, i : i + 1], scalar2=None, op0=ALU.mult
                     )
                 else:
-                    nc.scalar.activation(
-                        out=o_sb[:, i, h, :], in_=o_ps[:, i, :], func=ACT.Copy, scale=rden[:, i : i + 1]
-                    )
+                    nc.scalar.activation(out=o_sb[:, i, h, :], in_=o_in, func=ACT.Copy, scale=rden[:, i : i + 1])
             if b == B - 1 and tp == 1:
                 nc.sync.dma_start(
                     out=out[b].rearrange("(p t) h d -> p t h d", t=NT)[:, 2 * tp : 2 * tp + 2, h, :],
@@ -401,53 +418,56 @@ def tile_deepseekv4attention_t_kernel(tc, query, key, value, attention_mask, sin
         ident_b = const.tile([P, P], BF16)
         make_identity(nc, ident_b[:])
         ident16 = const.tile([P, P], BF16)
-        nc.vector.tensor_scalar(out=ident16[:], in0=ident_b[:], scalar1=1.0 / SCALE, scalar2=None, op0=ALU.mult)
+        nc.gpsimd.tensor_scalar(
+            out=ident16[:], in0=ident_b[:], scalar1=1.0 / SCALE, scalar2=0.0, op0=ALU.mult, op1=ALU.add
+        )
         sink_f = const.tile([P, H], F32)
         nc.vector.tensor_copy(out=sink_f[:], in_=sink_raw[:])
         nsink = const.tile([P, H], F32)
         nc.vector.tensor_scalar(out=nsink[:], in0=sink_raw[:], scalar1=-1.0, scalar2=None, op0=ALU.mult)
-        s_bufs = []
-        for h in range(H):
-            s_h = const.tile([P, 2, ROW], F32, name="s_h%d" % h)
-            for i in range(2):
-                nc.vector.memset(s_h[:, i, S:ROW], FILL)
-                nc.vector.tensor_copy(out=s_h[:, i, S : S + 1], in_=sink_raw[:, h : h + 1])
-            s_bufs.append(s_h)
+        s_all = const.tile([P, H, 2, ROW], F32)
+        nc.vector.memset(s_all[:, :, :, S:ROW], FILL)
+        for i in range(2):
+            nc.vector.tensor_copy(out=s_all[:, :, i, S], in_=sink_raw[:])
 
 
         prep_alloc(0)
         for x in range(V_PIECES):
             value_piece(0, x, None)
-        for m in range(-1, N_UNITS + 4):
+        for m in range(-1, N_UNITS + 5):
             b, j = divmod(m, UNITS_PER_BATCH)
             if valid(m) and j == 0 and b + 2 < B:
                 load(b + 2, False)
             if valid(m) and j == 0 and b + 1 < B:
                 prep_alloc(b + 1)
+            finish(m - 5)
             exps(m - 1)
+            b1, c1 = divmod(m - 1, UNITS_PER_BATCH)
+            c1 -= FIRST_PIECE_ROUND
+            copy_piece = valid(m - 1) and b1 + 1 < B and 0 <= c1 < len(PIECES)
+            if copy_piece and c1 not in VECTOR_PIECES:
+                words_copy(b1 + 1, PIECES[c1], False)
+            e_out_of_psum(m - 2)
             add_mask(m, 0)
             add_mask(m, 1)
-            if valid(m - 1):
-                b1, j1 = divmod(m - 1, UNITS_PER_BATCH)
-                c1 = j1 - FIRST_GROUP_ROUND
-                words_copy(b1 + 1, c1, c1 in VECTOR_GROUPS)
-            for c in FIRST_NEED.get(m + 1, ()):
-                words_transpose(0, c)
-                words_copy(0, c, c == 1)
+            for x in FIRST_NEED.get(m + 1, ()):
+                words_transpose(0, FIRST_PIECES[x])
+                words_copy(0, FIRST_PIECES[x], x in FIRST_BY_VECTOR)
             qk(m + 1, 0)
             pv(m - 4)
             qk(m + 1, 1)
             if valid(m):
                 value_piece(b + 1, j, st[(m - 1, "negm")][:] if valid(m - 1) else None)
-            e_out_of_psum(m - 2)
             e_transposes(m - 1)
-            finish(m - 4)
             if m == 2:
                 value_quant(0)
             if valid(m) and j == 0 and b > 0:
                 value_quant(b)
             e_quant(m - 3)
+            if copy_piece and c1 in VECTOR_PIECES:
+                words_copy(b1 + 1, PIECES[c1], True)
             recip(m - 2)
             row_max(m)
-            if valid(m):
-                words_transpose(b + 1, j - FIRST_GROUP_ROUND)
+            c = j - FIRST_PIECE_ROUND
+            if valid(m) and b + 1 < B and 0 <= c < len(PIECES):
+                words_transpose(b + 1, PIECES[c])

@@ -37,9 +37,10 @@ FIRST_PIECES = (
     ("q", 0, 2, 2, 2),
     ("q", 2, 2, 2, 2),
 )
-FIRST_NEED = {0: (0, 1), 1: (2, 3, 4), 2: (5,), 3: (6,)}
+FIRST_NEED = {0: (0, 1, 2), 1: (3, 4, 5, 6)}
 FIRST_BY_VECTOR = (1, 2)
 FIRST_PIECE_ROUND = 2
+FIRST_VALUE_ROUND = 3
 V_PIECES = 8
 N_LATE = 7
 PE_UNITS = (1, 4, 7)
@@ -143,7 +144,7 @@ def tile_deepseekv4attention_t_kernel(tc, query, key, value, attention_mask, sin
             which, h0, nh, t0, nt = piece
             src = loaded[b][which]
             if b == 0:
-                pool, tag = ((ps_tq, "tq"), (ps_et, "et"), (ps_o, "o_ps"))[FIRST_PIECES.index(piece) % 3]
+                pool, tag = ((ps_tq, "tq"), (ps_et, "et"), (ps_o, "o_ps"), (ps_et, "et"))[FIRST_PIECES.index(piece) % 4]
                 tq = pool.tile([P, NT, P], F32, tag=tag)
             else:
                 tq = ps_tq.tile([P, NT, P], F32, tag="tq")
@@ -170,14 +171,9 @@ def tile_deepseekv4attention_t_kernel(tc, query, key, value, attention_mask, sin
             else:
                 nc.scalar.copy(out=dst, in_=src)
 
-        def value_piece(b, x, pace):
-            if b >= B:
-                return
+        def value_piece(b, x):
             g, y = divmod(x, V_PIECES // HKV)
             wd = D * HKV // V_PIECES
-            if pace is not None:
-                seen = stat.tile([P, 2], F32, tag="seen")
-                nc.gpsimd.tensor_scalar(out=seen[:], in0=pace, scalar1=1.0, scalar2=0.0, op0=ALU.mult, op1=ALU.add)
             src = loaded[b]["v"][:, g * NT * D : (g + 1) * NT * D].rearrange("p (t d) -> p t d", t=NT)
             nc.gpsimd.tensor_scalar(
                 out=ready[b]["vg"][:, x * wd * NT : (x + 1) * wd * NT].rearrange("p (d t) -> p d t", t=NT),
@@ -433,7 +429,7 @@ def tile_deepseekv4attention_t_kernel(tc, query, key, value, attention_mask, sin
 
         prep_alloc(0)
         for x in range(V_PIECES):
-            value_piece(0, x, None)
+            value_piece(0, x)
         for m in range(-1, N_UNITS + 5):
             b, j = divmod(m, UNITS_PER_BATCH)
             if valid(m) and j == 0 and b + 2 < B:
@@ -456,8 +452,6 @@ def tile_deepseekv4attention_t_kernel(tc, query, key, value, attention_mask, sin
             qk(m + 1, 0)
             pv(m - 4)
             qk(m + 1, 1)
-            if valid(m):
-                value_piece(b + 1, j, st[(m - 1, "negm")][:] if valid(m - 1) else None)
             e_transposes(m - 1)
             if m == 2:
                 value_quant(0)
@@ -466,6 +460,12 @@ def tile_deepseekv4attention_t_kernel(tc, query, key, value, attention_mask, sin
             e_quant(m - 3)
             if copy_piece and c1 in VECTOR_PIECES:
                 words_copy(b1 + 1, PIECES[c1], True)
+            x = 2 * (j - FIRST_VALUE_ROUND)
+            if valid(m) and b + 1 < B and 0 <= x < V_PIECES:
+                seen = stat.tile([P, 1], U32, tag="seen")
+                nc.gpsimd.tensor_copy(out=seen[:], in_=st[(m - 3, "ec")][:, 0:1])
+                value_piece(b + 1, x)
+                value_piece(b + 1, x + 1)
             recip(m - 2)
             row_max(m)
             c = j - FIRST_PIECE_ROUND

from contextlib import ExitStack

import concourse.mybir as mybir
from concourse.masks import make_identity

F32 = mybir.dt.float32
BF16 = mybir.dt.bfloat16
U32 = mybir.dt.uint32
U8 = mybir.dt.uint8
FP8X4 = mybir.dt.float8_e4m3fn_x4
ALU = mybir.AluOpType
ACT = mybir.ActivationFunctionType
AX = mybir.AxisListType

B, H, HKV, S, D = 8, 4, 2, 512, 256
G = H // HKV
P = 128
NT = S // P
W = D // 2
SCALE = 1.0 / 16.0
ROW = 520
EXT = S + 4
FILL = -1.0e30
UNITS_PER_BATCH = H * NT // 2
N_UNITS = B * UNITS_PER_BATCH
TILE_E = P * NT
E_HALF = EXT // 2
DEN_STEP = 8
PIECES = (("k", 0, 1, 0, 4), ("q", 0, 1, 0, 4), ("q", 1, 1, 0, 4), ("k", 1, 1, 0, 4), ("q", 2, 1, 0, 4), ("q", 3, 1, 0, 4))
VECTOR_PIECES = (1, 4)
FIRST_PIECES = (
    ("k", 0, 1, 0, 4),
    ("q", 0, 1, 0, 2),
    ("q", 1, 1, 0, 2),
    ("k", 1, 1, 0, 4),
    ("q", 2, 2, 0, 2),
    ("q", 0, 2, 2, 2),
    ("q", 2, 2, 2, 2),
)
FIRST_NEED = {0: (0, 1, 2), 1: (3, 4, 5, 6)}
FIRST_BY_VECTOR = (1, 2)
FIRST_PIECE_ROUND = 2
FIRST_VALUE_ROUND = 3
V_PIECES = 8
N_LATE = 7
PE_UNITS = (1, 4, 7)
FLOPS = 2 * 2 * B * H * S * S * D


def tile_deepseekv4attention_t_kernel(tc, query, key, value, attention_mask, sinks, out):
    nc = tc.nc
    with ExitStack() as ctx:
        const = ctx.enter_context(tc.tile_pool(name="const", bufs=1))
        ld = ctx.enter_context(tc.tile_pool(name="ld", bufs=3))
        prep = ctx.enter_context(tc.tile_pool(name="prep", bufs=2))
        prep3 = ctx.enter_context(tc.tile_pool(name="prep3", bufs=3))
        work = ctx.enter_context(tc.tile_pool(name="work", bufs=3))
        work4 = ctx.enter_context(tc.tile_pool(name="work4", bufs=4))
        stat = ctx.enter_context(tc.tile_pool(name="stat", bufs=6))
        outp = ctx.enter_context(tc.tile_pool(name="outp", bufs=3))
        ps_sc = ctx.enter_context(tc.psum_pool(name="ps_sc", bufs=4))
        ps_et = ctx.enter_context(tc.psum_pool(name="ps_et", bufs=2))
        ps_o = ctx.enter_context(tc.psum_pool(name="ps_o", bufs=1))
        ps_tq = ctx.enter_context(tc.psum_pool(name="ps_tq", bufs=1))
        ctx.enter_context(tc.manual_schedule())

        loaded = {}
        ready = {}
        st = {}

        def valid(n):
            return 0 <= n < N_UNITS

        def where(n):
            b, j = divmod(n, UNITS_PER_BATCH)
            tp, h = divmod(j, H)
            return b, tp, h

        def mask_on_pe(n, i):
            return i == 1 and n % UNITS_PER_BATCH in PE_UNITS or n == N_UNITS - 1

        def mask_tile(b, t):
            return loaded[b]["m"][:, t * S : (t + 1) * S]

        def late(n):
            return n >= N_UNITS - N_LATE


        def load(b, fine):
            k_sb = ld.tile([P, HKV * NT * D], BF16, tag="k_sb")
            q_sb = ld.tile([P, H * NT * D], BF16, tag="q_sb")
            m_sb = ld.tile([P, NT * S], BF16, tag="m_sb")
            v_sb = ld.tile([P, HKV * NT * D], BF16, tag="v_sb")
            loaded[b] = {"q": q_sb, "k": k_sb, "v": v_sb, "m": m_sb}
            blk = NT * D

            def load_k(g0, g1):
                nc.sync.dma_start(
                    out=k_sb[:, g0 * blk : g1 * blk].rearrange("p (g x) -> p g x", x=blk),
                    in_=key[b, g0:g1].rearrange("g (p t) d -> p g (t d)", t=NT),
                )

            def load_q(tp, h0, h1):
                nc.sync.dma_start(
                    out=q_sb[:].rearrange("p (a x) -> p a x", x=2 * D)[:, tp * H + h0 : tp * H + h1, :],
                    in_=query[b, h0:h1].rearrange("h (p t) d -> p h (t d)", t=NT)[:, :, tp * 2 * D : (tp + 1) * 2 * D],
                )

            def load_m(t0, t1):
                nc.sync.dma_start(
                    out=m_sb[:, t0 * S : t1 * S],
                    in_=attention_mask[b, 0].rearrange("(p t) k -> p t k", t=NT)[:, t0:t1, :].rearrange("p t k -> p (t k)"),
                )

            if fine:
                load_k(0, 1)
                load_q(0, 0, 1)
                load_q(0, 1, 2)
                load_m(0, 2)
                load_k(1, 2)
                load_q(0, 2, H)
                load_q(1, 0, H)
                load_m(2, NT)
            else:
                load_k(0, HKV)
                load_q(0, 0, H)
                load_q(1, 0, H)
                load_m(0, NT)
            nc.sync.dma_start(
                out=v_sb[:].rearrange("p (g x) -> p g x", x=blk),
                in_=value[b].rearrange("g (p t) d -> p g (t d)", t=NT),
            )


        def prep_alloc(b):
            qT = prep.tile([P, H * NT * P], F32, tag="qT")
            kT = prep.tile([P, HKV * NT * P], F32, tag="kT")
            vg = prep.tile([P, HKV * D * NT], BF16, tag="vg", align_bytes=64)
            vc = prep3.tile([P, HKV * D], U32, tag="vc", align_bytes=64)
            vs = prep3.tile([P, HKV * D], U8, tag="vs", align_bytes=64)
            ready[b] = {"q": qT, "k": kT, "vg": vg, "vc": vc, "vs": vs}

        def words_transpose(b, piece):
            which, h0, nh, t0, nt = piece
            src = loaded[b][which]
            if b == 0:
                pool, tag = ((ps_tq, "tq"), (ps_et, "et"), (ps_o, "o_ps"), (ps_et, "et"))[FIRST_PIECES.index(piece) % 4]
                tq = pool.tile([P, NT, P], F32, tag=tag)
            else:
                tq = ps_tq.tile([P, NT, P], F32, tag="tq")
            for x in range(nh * nt):
                hx, tx = h0 + x // nt, t0 + x % nt
                if which == "k":
                    c0 = (hx * NT + tx) * W
                else:
                    c0 = ((tx // 2 * H + hx) * 2 + tx % 2) * W
                nc.tensor.transpose(tq[:, x, :], src[:].bitcast(F32)[:, c0 : c0 + W], ident_f[:])
            st[(b, "tq", piece)] = tq

        def words_copy(b, piece, on_vector):
            which, h0, nh, t0, nt = piece
            tq = st[(b, "tq", piece)]
            if which == "k":
                dst = ready[b]["k"][:, h0 * S : (h0 + 1) * S].rearrange("p (r t) -> p r t", t=NT)
                src = tq[:].rearrange("p t r -> p r t")
            else:
                dst = ready[b]["q"][:].rearrange("p (h x) -> p h x", h=H)[:, h0 : h0 + nh, t0 * P : (t0 + nt) * P]
                src = tq[:, 0 : nh * nt, :].rearrange("p (h t) r -> p h (t r)", h=nh)
            if on_vector:
                nc.vector.tensor_copy(out=dst, in_=src)
            else:
                nc.scalar.copy(out=dst, in_=src)

        def value_piece(b, x):
            g, y = divmod(x, V_PIECES // HKV)
            wd = D * HKV // V_PIECES
            src = loaded[b]["v"][:, g * NT * D : (g + 1) * NT * D].rearrange("p (t d) -> p t d", t=NT)
            nc.gpsimd.tensor_scalar(
                out=ready[b]["vg"][:, x * wd * NT : (x + 1) * wd * NT].rearrange("p (d t) -> p d t", t=NT),
                in0=src[:, :, y * wd : (y + 1) * wd].rearrange("p t d -> p d t"),
                scalar1=1.0,
                scalar2=0.0,
                op0=ALU.mult,
                op1=ALU.add,
            )

        def value_quant(b):
            if b >= B:
                return
            r = ready[b]
            nc.vector.quantize_mx(out=r["vc"][:].bitcast(FP8X4), scales=r["vs"][:], in_=r["vg"][:])


        def qk(n, i):
            if not valid(n):
                return
            b, tp, h = where(n)
            g = h // G
            t = 2 * tp + i
            qTb = ready[b]["q"][:].bitcast(BF16).rearrange("p (c e) -> p c e", e=2)
            kTb = ready[b]["k"][:].bitcast(BF16).rearrange("p (c e) -> p c e", e=2)
            sc = ps_sc.tile([P, S], F32, tag="sc")
            c0 = (h * NT + t) * P
            on_pe = mask_on_pe(n, i)
            if on_pe:
                nc.tensor.matmul(
                    sc[:], lhsT=ident16[:], rhs=mask_tile(b, t), start=True, stop=False
                )
            for e in range(2):
                nc.tensor.matmul(
                    sc[:],
                    lhsT=qTb[:, c0 : c0 + P, e],
                    rhs=kTb[:, g * S : (g + 1) * S, e],
                    start=(e == 0 and not on_pe),
                    stop=(e == 1),
                )
            st[(n, "sc", i)] = sc

        def add_mask(n, i):
            if not valid(n):
                return
            b, tp, h = where(n)
            t = 2 * tp + i
            if i == 0:
                negm = stat.tile([P, 2], F32, tag="negm")
                st[(n, "negm")] = negm
            if mask_on_pe(n, i):
                minus_s = work.tile([P, S], BF16, tag="minus_s")
                nc.vector.tensor_scalar(
                    out=minus_s[:],
                    in0=st[(n, "sc", i)][:],
                    scalar1=-SCALE,
                    scalar2=nsink[:, h : h + 1],
                    op0=ALU.mult,
                    op1=ALU.min,
                    accum_out=st[(n, "negm")][:, i : i + 1],
                )
                return
            nc.vector.scalar_tensor_tensor(
                out=s_all[:, h, i, 0:S],
                in0=st[(n, "sc", i)][:],
                scalar=SCALE,
                in1=mask_tile(b, t),
                op0=ALU.mult,
                op1=ALU.add,
            )

        def row_max(n):
            if not valid(n):
                return
            b, tp, h = where(n)
            k = sum(not mask_on_pe(n, i) for i in range(2))
            if k > 0:
                nc.vector.tensor_reduce(
                    out=st[(n, "negm")][:, 0:k], in_=s_all[:, h, 0:k, 0 : S + 1], axis=AX.X, op=ALU.max, negate=True
                )

        def exps(n):
            if not valid(n):
                return
            b, tp, h = where(n)
            negm = st[(n, "negm")]
            e_sb = work.tile([P, 2, 2, E_HALF], BF16, tag="e_sb")
            if n % 2 == 0:
                den_pair = stat.tile([P, 2 * DEN_STEP], F32, tag="den_pair")
                st[(n // 2, "den_pair")] = den_pair
            c_den = (n % 2) * DEN_STEP
            den = st[(n // 2, "den_pair")][:, c_den : c_den + 2]
            for i in (1, 0) if mask_on_pe(n, 1) and not mask_on_pe(n, 0) else (0, 1):
                if mask_on_pe(n, i):
                    e_sum = stat.tile([P, 1], F32, tag="e_sum")
                    nc.scalar.activation(
                        out=e_sb[:, i, :, 0 : S // 2].rearrange("p u (w v) -> p u w v", v=2),
                        in_=st[(n, "sc", i)][:].rearrange("p (w u v) -> p u w v", u=2, v=2),
                        func=ACT.Exp,
                        bias=negm[:, i : i + 1],
                        scale=SCALE,
                        accum_out=e_sum[:],
                    )
                    e_sink = stat.tile([P, 1], F32, tag="e_sink")
                    nc.scalar.activation(
                        out=e_sink[:], in_=negm[:, i : i + 1], func=ACT.Exp, bias=sink_f[:, h : h + 1], scale=1.0
                    )
                    nc.gpsimd.tensor_tensor(out=den[:, i : i + 1], in0=e_sum[:], in1=e_sink[:], op=ALU.add)
                else:
                    nc.scalar.activation(
                        out=e_sb[:, i, :, :].rearrange("p u (w v) -> p u w v", v=2),
                        in_=s_all[:, h, i, 0:EXT].rearrange("p (w u v) -> p u w v", u=2, v=2),
                        func=ACT.Exp,
                        bias=negm[:, i : i + 1],
                        scale=1.0,
                        accum_out=den[:, i : i + 1],
                    )
            st[(n, "e")] = e_sb

        def recip(n):
            if not valid(n):
                return
            den_pair = st[(n // 2, "den_pair")]
            if n % 2 == 1:
                rden = stat.tile([P, 2, 2], F32, tag="rden")
                nc.vector.reciprocal(out=rden[:], in_=den_pair[:].rearrange("p (a x) -> p a x", x=DEN_STEP)[:, :, 0:2])
                st[(n // 2, "rden")] = rden

        def parts(n):
            return ((0,), (1,)) if n == N_UNITS - 1 else ((0, 1),)

        def e_transposes(n):
            if not valid(n):
                return
            e_sb = st[(n, "e")]
            for part in parts(n):
                et = ps_et.tile([P, 2, 2, P], F32, tag="et")
                for x, i in enumerate(part):
                    for u in range(2):
                        nc.tensor.transpose(et[:, x, u, :], e_sb[:, i, u, 0 : S // 2].bitcast(F32), ident_f[:])
                st[(n, "et", part)] = et

        def e_out_of_psum(n):
            if not valid(n):
                return
            gr = work4.tile([P, 2 * TILE_E], BF16, tag="gr", align_bytes=64)
            st[(n, "gr")] = gr
            for part in parts(n):
                k = len(part)
                out_words = (
                    gr[:, part[0] * TILE_E : (part[-1] + 1) * TILE_E]
                    .bitcast(F32)
                    .rearrange("p (i q u) -> p i q u", i=k, u=2)
                )
                in_words = st[(n, "et", part)][:, 0:k].rearrange("p i u q -> p i q u")
                if n >= N_UNITS - 2 and part[0] == 0:
                    nc.vector.tensor_copy(out=out_words, in_=in_words)
                else:
                    nc.scalar.copy(out=out_words, in_=in_words)

        def e_quant(n):
            if not valid(n):
                return
            ec = work.tile([P, 2 * P], U32, tag="ec", align_bytes=64)
            es = work.tile([P, 2 * P], U8, tag="es", align_bytes=64)
            for part in parts(n):
                cols = slice(part[0] * P, (part[-1] + 1) * P)
                nc.vector.quantize_mx(
                    out=ec[:, cols].bitcast(FP8X4),
                    scales=es[:, cols],
                    in_=st[(n, "gr")][:, part[0] * TILE_E : (part[-1] + 1) * TILE_E],
                )
            st[(n, "ec")] = ec
            st[(n, "es")] = es

        def pv(n):
            if not valid(n):
                return
            b, tp, h = where(n)
            g = h // G
            vc = ready[b]["vc"]
            vs = ready[b]["vs"]
            ec = st[(n, "ec")]
            es = st[(n, "es")]
            for part in parts(n):
                if late(n):
                    o_ps = ps_sc.tile([P, 2, D], F32, tag="sc")
                else:
                    o_ps = ps_o.tile([P, 2, D], F32, tag="o_ps")
                for x, i in enumerate(part):
                    cols = slice(i * P, (i + 1) * P)
                    nc.tensor.matmul_mx(
                        out=o_ps[:, x, :],
                        lhsT=ec[:, cols].bitcast(FP8X4),
                        lhsT_scale=es[:, cols],
                        rhs=vc[:, g * D : (g + 1) * D].bitcast(FP8X4),
                        rhs_scale=vs[:, g * D : (g + 1) * D],
                        start=True,
                        stop=True,
                    )
                    st[(n, "o", i)] = o_ps[:, x, :]

        def finish(n):
            if not valid(n):
                return
            b, tp, h = where(n)
            rden = st[(n // 2, "rden")][:, n % 2, :]
            if h == 0:
                o_new = outp.tile([P, 2, H, D], F32, tag="o_sb")
                st[(b, tp, "o_sb")] = o_new
            o_sb = st[(b, tp, "o_sb")]
            for i in range(2):
                o_in = st[(n, "o", i)]
                if late(n) and (i == 0 or n < N_UNITS - 1):
                    nc.vector.tensor_scalar(
                        out=o_sb[:, i, h, :], in0=o_in, scalar1=rden[:, i : i + 1], scalar2=None, op0=ALU.mult
                    )
                else:
                    nc.scalar.activation(out=o_sb[:, i, h, :], in_=o_in, func=ACT.Copy, scale=rden[:, i : i + 1])
            if b == B - 1 and tp == 1:
                nc.sync.dma_start(
                    out=out[b].rearrange("(p t) h d -> p t h d", t=NT)[:, 2 * tp : 2 * tp + 2, h, :],
                    in_=o_sb[:, :, h, :],
                )
            elif h == H - 1:
                nc.sync.dma_start(
                    out=out[b].rearrange("(p t) h d -> p t (h d)", t=NT)[:, 2 * tp : 2 * tp + 2, :],
                    in_=o_sb[:].rearrange("p i h d -> p i (h d)"),
                )


        sink_raw = const.tile([P, H], BF16)
        nc.scalar.dma_start(out=sink_raw[:], in_=sinks.partition_broadcast(P))
        load(0, True)
        load(1, False)
        ident_f = const.tile([P, P], F32)
        make_identity(nc, ident_f[:])
        ident_b = const.tile([P, P], BF16)
        make_identity(nc, ident_b[:])
        ident16 = const.tile([P, P], BF16)
        nc.gpsimd.tensor_scalar(
            out=ident16[:], in0=ident_b[:], scalar1=1.0 / SCALE, scalar2=0.0, op0=ALU.mult, op1=ALU.add
        )
        sink_f = const.tile([P, H], F32)
        nc.vector.tensor_copy(out=sink_f[:], in_=sink_raw[:])
        nsink = const.tile([P, H], F32)
        nc.vector.tensor_scalar(out=nsink[:], in0=sink_raw[:], scalar1=-1.0, scalar2=None, op0=ALU.mult)
        s_all = const.tile([P, H, 2, ROW], F32)
        nc.vector.memset(s_all[:, :, :, S:ROW], FILL)
        for i in range(2):
            nc.vector.tensor_copy(out=s_all[:, :, i, S], in_=sink_raw[:])


        prep_alloc(0)
        for x in range(V_PIECES):
            value_piece(0, x)
        for m in range(-1, N_UNITS + 5):
            b, j = divmod(m, UNITS_PER_BATCH)
            if valid(m) and j == 0 and b + 2 < B:
                load(b + 2, False)
            if valid(m) and j == 0 and b + 1 < B:
                prep_alloc(b + 1)
            finish(m - 5)
            exps(m - 1)
            b1, c1 = divmod(m - 1, UNITS_PER_BATCH)
            c1 -= FIRST_PIECE_ROUND
            copy_piece = valid(m - 1) and b1 + 1 < B and 0 <= c1 < len(PIECES)
            if copy_piece and c1 not in VECTOR_PIECES:
                words_copy(b1 + 1, PIECES[c1], False)
            e_out_of_psum(m - 2)
            add_mask(m, 0)
            add_mask(m, 1)
            for x in FIRST_NEED.get(m + 1, ()):
                words_transpose(0, FIRST_PIECES[x])
                words_copy(0, FIRST_PIECES[x], x in FIRST_BY_VECTOR)
            qk(m + 1, 0)
            pv(m - 4)
            qk(m + 1, 1)
            e_transposes(m - 1)
            if m == 2:
                value_quant(0)
            if valid(m) and j == 0 and b > 0:
                value_quant(b)
            e_quant(m - 3)
            if copy_piece and c1 in VECTOR_PIECES:
                words_copy(b1 + 1, PIECES[c1], True)
            x = 2 * (j - FIRST_VALUE_ROUND)
            if valid(m) and b + 1 < B and 0 <= x < V_PIECES:
                seen = stat.tile([P, 1], U32, tag="seen")
                nc.gpsimd.tensor_copy(out=seen[:], in_=st[(m - 3, "ec")][:, 0:1])
                value_piece(b + 1, x)
                value_piece(b + 1, x + 1)
            recip(m - 2)
            row_max(m)
            c = j - FIRST_PIECE_ROUND
            if valid(m) and b + 1 < B and 0 <= c < len(PIECES):
                words_transpose(b + 1, PIECES[c])
